import numpy as np
import ml_dtypes


def mxq(x, axis, fmt="e4m3"):
    dtype, down = {"e4m3": (ml_dtypes.float8_e4m3fn, 7), "e5m2": (ml_dtypes.float8_e5m2, 14)}[fmt]
    v = np.moveaxis(np.asarray(x, np.float32).astype(ml_dtypes.bfloat16).astype(np.float64), axis, -1)
    blocks = v.reshape(v.shape[:-1] + (-1, 32))
    amax = np.abs(blocks).max(-1, keepdims=True)
    byte = np.maximum(np.where(amax > 0, np.frexp(amax)[1] - 1 + 127, 0) - down, 1)
    scale = np.exp2(byte - 127.0)
    codes = (blocks / scale).astype(np.float32).astype(dtype).astype(np.float64)
    return np.moveaxis((codes * scale).reshape(v.shape), -1, axis)


WIDE = False


def mx_kscale(k):
    if not WIDE:
        return np.ones(k)
    levels = np.array([10, -10, 5, -5, 0])
    a = np.random.permutation(np.resize(levels, k // 512 * 4)).reshape(k // 512, 4)
    idx = np.arange(k)
    return np.exp2(a[idx // 512, idx % 128 // 32])


BF16 = ml_dtypes.bfloat16


def bf(x):
    return np.asarray(x, np.float32).astype(BF16)


def f64(x):
    return np.asarray(x).astype(np.float64)


E2M1 = np.array([0.0, 0.5, 1.0, 1.5, 2.0, 3.0, 4.0, 6.0, -0.0, -0.5, -1.0, -1.5, -2.0, -3.0, -4.0, -6.0])


def pack_weight(w, fmt):
    k, n = w.shape
    w = f64(bf(w)).reshape(k // 32, 32, n)
    amax = np.abs(w).max(1)
    if fmt == "e4m3":
        byte = np.frexp(amax)[1] - 1 + 127 - 7
    else:
        mant, ex = np.frexp(amax / 6.0)
        byte = np.where(mant > 0.5, ex, ex - 1) + 127
    byte = np.clip(np.where(amax > 0, byte, 1), 1, 254)
    scaled = (w * np.exp2(127.0 - byte)[:, None, :]).reshape(k, n).astype(np.float32)
    by_word = np.ascontiguousarray(scaled.reshape(k // 512, 128, 4, n).transpose(0, 1, 3, 2))
    if fmt == "e4m3":
        words = by_word.astype(ml_dtypes.float8_e4m3fn).view(np.uint8)
    else:
        c = by_word.astype(ml_dtypes.float4_e2m1fn).view(np.uint8) & 0xF
        words = c[..., 0::2] | (c[..., 1::2] << 4)
    return np.ascontiguousarray(words), np.ascontiguousarray(byte.astype(np.uint8).reshape(k // 512, 16, n))


def unpack_weight(words, scales, fmt):
    g, p, n, _ = words.shape
    if fmt == "e4m3":
        vals = np.ascontiguousarray(words).view(ml_dtypes.float8_e4m3fn).astype(np.float64)
    else:
        nib = np.empty((g, p, n, 4), np.uint8)
        nib[..., 0::2] = words & 0xF
        nib[..., 1::2] = words >> 4
        vals = E2M1[nib]
    vals = vals * np.repeat(np.exp2(scales.astype(np.float64) - 127.0), 8, axis=1)[..., None]
    return vals.transpose(0, 1, 3, 2).reshape(g * 512, n)


B, L, DIM, H, D = 2, 64, 8192, 16, 64
EPS = 1e-6
THETA = 10000.0
FMT = "e4m3"


def rope_table(seq_len, head_dim):
    pos = np.arange(seq_len, dtype=np.float64)
    inv = 1.0 / (THETA ** (np.arange(0, head_dim, 2, dtype=np.float64) / head_dim))
    ang = pos[:, None] * inv[None, :]
    cos, sin = np.cos(ang), np.sin(ang)
    rot = np.stack([np.stack([cos, -sin], -1), np.stack([sin, cos], -1)], -2)
    return rot[None, None]


def rms_norm(u, gain):
    rrms = 1.0 / np.sqrt(np.mean(np.square(u), axis=-1, keepdims=True) + EPS)
    return u * rrms * gain


def rope(u, table):
    ur = u.reshape(*u.shape[:-1], -1, 1, 2)
    out = table[..., 0] * ur[..., 0] + table[..., 1] * ur[..., 1]
    return out.reshape(u.shape)


def setup_inputs():
    s = mx_kscale(DIM)
    x = bf(np.random.standard_normal((B, L, DIM)) * s)
    pe = bf(rope_table(L, D))
    words, scales = pack_weight(np.random.standard_normal((DIM, 3 * H * D)) / np.sqrt(DIM) / s[:, None], FMT)
    qkv_b = bf(np.random.standard_normal(3 * H * D) * 0.2)
    q_scale = bf(1.0 + 0.1 * np.random.standard_normal(D))
    k_scale = bf(1.0 + 0.1 * np.random.standard_normal(D))
    return {"x": x,
            "pe": pe,
            "qkv_w_words": words,
            "qkv_w_scales": scales,
            "qkv_b": qkv_b,
            "q_scale": q_scale,
            "k_scale": k_scale}


def reference(x, pe, qkv_w_words, qkv_w_scales, qkv_b, q_scale, k_scale):
    qkv = (mxq(f64(x), 2, "e4m3") @ unpack_weight(qkv_w_words, qkv_w_scales, FMT)) + f64(qkv_b)
    qkv = qkv.reshape(B, L, 3, H, D).transpose(2, 0, 3, 1, 4)
    q, k, v = qkv[0], qkv[1], qkv[2]
    q = rms_norm(q, f64(q_scale))
    k = rms_norm(k, f64(k_scale))
    table = f64(pe)
    return rope(q, table), rope(k, table), v

@@ -1,0 +1,278 @@
+from contextlib import ExitStack
+
+import concourse.mybir as mybir
+from concourse.masks import make_identity
+
+BF16 = mybir.dt.bfloat16
+F32 = mybir.dt.float32
+I32 = mybir.dt.int32
+U32 = mybir.dt.uint32
+U8 = mybir.dt.uint8
+FP8X4 = mybir.dt.float8_e4m3fn_x4
+ADD = mybir.AluOpType.add
+MULT = mybir.AluOpType.mult
+SQUARE = mybir.ActivationFunctionType.Square
+SQRT = mybir.ActivationFunctionType.Sqrt
+
+P = 128
+BATCHES = 2
+POSITIONS = 64
+HEADS = 16
+FEATURES = 64
+PAIRS = FEATURES // 2
+EPS = 1e-6
+
+PACK = 4
+K_GROUP = P * PACK
+K_ALL = 8192
+GROUPS = K_ALL // K_GROUP
+WORDS_PER_GROUP = K_GROUP // 2
+
+STREAMS = 3
+STREAM_COLS = HEADS * FEATURES
+N_ALL = STREAMS * STREAM_COLS
+BANK = 512
+BANKS_PER_STREAM = STREAM_COLS // BANK
+HEADS_PER_BANK = BANK // FEATURES
+
+X_CHUNKS = 4
+CHUNK_GROUPS = GROUPS // X_CHUNKS
+CHUNK_K = K_ALL // X_CHUNKS
+
+PLANES_PER_TILE = 4
+W_GROUPS_PER_LOAD = 2
+W_BUFS = 12
+
+ROW_COLS = N_ALL + BANK
+
+FLOPS = 2 * P * K_ALL * N_ALL
+
+
+def load_x(nc, x_pool, x):
+    x_rows = x.rearrange("b l k -> (b l) k")
+    x_chunks = []
+    for c in range(X_CHUNKS):
+        x_chunk = x_pool.tile([P, CHUNK_K], BF16)
+        nc.sync.dma_start(out=x_chunk[:], in_=x_rows[:, c * CHUNK_K : (c + 1) * CHUNK_K])
+        x_chunks.append(x_chunk)
+    return x_chunks
+
+
+def load_w_scales(nc, keep, qkv_w_scales):
+    w_planes = keep.tile([P, GROUPS // PLANES_PER_TILE, N_ALL], U8, align_bytes=64)
+    nc.vector.memset(w_planes[:].bitcast(I32), 0)
+    for j in range(GROUPS // PLANES_PER_TILE):
+        for quadrant in range(4):
+            nc.sync.dma_start(
+                out=w_planes[32 * quadrant : 32 * quadrant + 16, j, :].bitcast(I32),
+                in_=qkv_w_scales[
+                    PLANES_PER_TILE * j : PLANES_PER_TILE * (j + 1), 4 * quadrant : 4 * quadrant + 4, :
+                ].bitcast(I32),
+            )
+    return w_planes
+
+
+def quantise_x(nc, keep, grouped_pool, psum, x_chunks):
+    ident = keep.tile([P, P], F32)
+    make_identity(nc, ident[:])
+    x_codes = keep.tile([P, GROUPS, P], U32, align_bytes=64)
+    x_planes = keep.tile([P, GROUPS, P], U8, align_bytes=64)
+    for c in range(X_CHUNKS):
+        x_words = x_chunks[c][:].bitcast(F32)
+        grouped = grouped_pool.tile([P, CHUNK_GROUPS, P, PACK], BF16, align_bytes=64)
+        grouped_words = grouped[:].bitcast(F32)
+        for half in range(2):
+            turned = psum.tile([P, 2, 2, P], F32, tag="bank")
+            for gl in range(2):
+                first = WORDS_PER_GROUP * (2 * half + gl)
+                for u in range(2):
+                    nc.tensor.transpose(
+                        turned[:, gl, u, :], x_words[:, first + u : first + WORDS_PER_GROUP : 2], ident[:]
+                    )
+            side_by_side = turned[:].rearrange("p g u m -> p g m u")
+            if half == 0:
+                nc.vector.tensor_copy(out=grouped_words[:, 0:2, :, :], in_=side_by_side)
+            else:
+                nc.scalar.copy(out=grouped_words[:, 2:4, :, :], in_=side_by_side)
+        groups = slice(c * CHUNK_GROUPS, (c + 1) * CHUNK_GROUPS)
+        nc.vector.quantize_mx(
+            out=x_codes[:, groups, :].rearrange("p g m -> p (g m)").bitcast(FP8X4),
+            scales=x_planes[:, groups, :].rearrange("p g m -> p (g m)"),
+            in_=grouped[:].rearrange("p g m t -> p (g m t)"),
+        )
+    return x_codes, x_planes
+
+
+def spread_constants(nc, keep, psum, pe, qkv_b, q_scale, k_scale):
+    row = keep.tile([P, ROW_COLS], BF16)
+    nc.vector.memset(row[:], 0.0)
+    ones = keep.tile([P, P], BF16)
+    nc.vector.memset(ones[:], 1.0)
+    nc.scalar.dma_start(out=row[0:1, 0:N_ALL], in_=qkv_b.rearrange("(o n) -> o n", o=1))
+    nc.scalar.dma_start(out=row[0:1, N_ALL : N_ALL + FEATURES], in_=q_scale.rearrange("(o n) -> o n", o=1))
+    nc.scalar.dma_start(
+        out=row[0:1, N_ALL + FEATURES : N_ALL + 2 * FEATURES], in_=k_scale.rearrange("(o n) -> o n", o=1)
+    )
+    pe_sb = keep.tile([P, PAIRS * 4], BF16)
+    for b in range(BATCHES):
+        nc.scalar.dma_start(
+            out=pe_sb[b * POSITIONS : (b + 1) * POSITIONS, :],
+            in_=pe.rearrange("a b l i r c -> (a b l) (i r c)"),
+        )
+
+    bias_planes = keep.tile([P, 2, 2, HEADS, PAIRS], F32)
+    bias_v = keep.tile([P, STREAM_COLS], F32)
+    tables = keep.tile([P, 2, 2, 2, PAIRS], F32)
+    for t in range(ROW_COLS // BANK):
+        spread = psum.tile([P, BANK], F32, tag="bank")
+        nc.tensor.matmul(out=spread[:], lhsT=ones[:], rhs=row[:, t * BANK : (t + 1) * BANK], start=True, stop=True)
+        stream = t // BANKS_PER_STREAM
+        j = t % BANKS_PER_STREAM
+        if stream < 2:
+            nc.scalar.copy(
+                out=bias_planes[:, stream, :, j * HEADS_PER_BANK : (j + 1) * HEADS_PER_BANK, :],
+                in_=spread[:].rearrange("p (h i e) -> p e h i", i=PAIRS, e=2),
+            )
+        elif stream == 2:
+            nc.scalar.copy(out=bias_v[:, j * BANK : (j + 1) * BANK], in_=spread[:])
+        else:
+            for s in range(2):
+                gain = spread[:, s * FEATURES : (s + 1) * FEATURES].rearrange("p (i c) -> p c i", c=2)
+                nc.vector.tensor_tensor(
+                    out=tables[:, s],
+                    in0=pe_sb[:].rearrange("p (i r c) -> p c r i", r=2, c=2),
+                    in1=gain.unsqueeze(2).to_broadcast([P, 2, 2, PAIRS]),
+                    op=MULT,
+                )
+    return bias_planes, bias_v, tables
+
+
+def project(nc, w_pool, psum, qkv_w_words, w_planes, x_codes, x_planes, stream):
+    first_col = stream * STREAM_COLS
+    w_rows = qkv_w_words.rearrange("g p n t -> p g (n t)")
+    acc = []
+    for j in range(BANKS_PER_STREAM):
+        bank = psum.tile([P, BANK], F32, tag="bank")
+        acc.append(bank)
+    for load in range(GROUPS // W_GROUPS_PER_LOAD):
+        first_group = load * W_GROUPS_PER_LOAD
+        w_words = w_pool.tile([P, W_GROUPS_PER_LOAD, STREAM_COLS], U32, align_bytes=64)
+        nc.sync.dma_start(
+            out=w_words[:].bitcast(I32),
+            in_=w_rows[
+                :, first_group : first_group + W_GROUPS_PER_LOAD, PACK * first_col : PACK * (first_col + STREAM_COLS)
+            ].bitcast(I32),
+        )
+        for j in range(BANKS_PER_STREAM):
+            for gl in range(W_GROUPS_PER_LOAD):
+                g = first_group + gl
+                plane_start = 4 * (g % PLANES_PER_TILE)
+                nc.tensor.matmul_mx(
+                    out=acc[j][:],
+                    lhsT=x_codes[:, g, :].bitcast(FP8X4),
+                    lhsT_scale=x_planes[:, g, :],
+                    rhs=w_words[:, gl, j * BANK : (j + 1) * BANK].bitcast(FP8X4),
+                    rhs_scale=w_planes[
+                        plane_start:P, g // PLANES_PER_TILE, first_col + j * BANK : first_col + (j + 1) * BANK
+                    ],
+                    start=(g == 0),
+                    stop=(g == GROUPS - 1),
+                )
+    return acc
+
+
+def store_heads(nc, out_dram, heads, rows):
+    for b in range(BATCHES):
+        nc.scalar.dma_start(
+            out=out_dram[b, heads].rearrange("h l d -> l h d"),
+            in_=rows[b * POSITIONS : (b + 1) * POSITIONS],
+        )
+
+
+def norm_and_rotate(nc, work, acc, bias_planes, table, out_dram):
+    planes_shape = [P, 2, HEADS, PAIRS]
+    biased = work.tile(planes_shape, F32)
+    for j in range(BANKS_PER_STREAM):
+        heads = slice(j * HEADS_PER_BANK, (j + 1) * HEADS_PER_BANK)
+        nc.vector.tensor_tensor(
+            out=biased[:, :, heads, :],
+            in0=acc[j][:].rearrange("p (h i e) -> p e h i", i=PAIRS, e=2),
+            in1=bias_planes[:, :, heads, :],
+            op=ADD,
+        )
+
+    squares = work.tile(planes_shape, F32)
+    nc.scalar.activation(out=squares[:], in_=biased[:], func=SQUARE)
+    sums = work.tile([P, HEADS], F32)
+    nc.vector.tensor_reduce(
+        out=sums[:], in_=squares[:].rearrange("p e h i -> p h e i"), axis=mybir.AxisListType.XY, op=ADD
+    )
+    mean_eps = work.tile([P, HEADS], F32)
+    nc.vector.tensor_scalar(
+        out=mean_eps[:], in0=sums[:], scalar1=1.0 / FEATURES, scalar2=EPS, op0=MULT, op1=ADD
+    )
+    rms = work.tile([P, HEADS], F32)
+    nc.scalar.activation(out=rms[:], in_=mean_eps[:], func=SQRT)
+    rrms = work.tile([P, HEADS], F32)
+    nc.vector.reciprocal(out=rrms[:], in_=rms[:])
+
+    normed = work.tile(planes_shape, F32)
+    nc.vector.tensor_tensor(
+        out=normed[:], in0=biased[:], in1=rrms[:].unsqueeze(1).unsqueeze(3).to_broadcast(planes_shape), op=MULT
+    )
+    from_plane = []
+    for c in range(2):
+        part = work.tile(planes_shape, F32, name="from_plane%d" % c)
+        nc.vector.tensor_tensor(
+            out=part[:],
+            in0=normed[:, c].unsqueeze(1).to_broadcast(planes_shape),
+            in1=table[:, c].unsqueeze(2).to_broadcast(planes_shape),
+            op=MULT,
+        )
+        from_plane.append(part)
+    rotated = work.tile([P, HEADS, PAIRS, 2], F32)
+    nc.vector.tensor_tensor(
+        out=rotated[:],
+        in0=from_plane[0][:].rearrange("p r h i -> p h i r"),
+        in1=from_plane[1][:].rearrange("p r h i -> p h i r"),
+        op=ADD,
+    )
+    store_heads(nc, out_dram, slice(0, HEADS), rotated[:].rearrange("p h i r -> p h (i r)"))
+
+
+def add_bias_to_v(nc, work, acc, bias_v, out_dram):
+    for j in range(BANKS_PER_STREAM):
+        v_rows = work.tile([P, BANK], F32, name="v_rows%d" % j)
+        nc.vector.tensor_tensor(out=v_rows[:], in0=acc[j][:], in1=bias_v[:, j * BANK : (j + 1) * BANK], op=ADD)
+        store_heads(
+            nc,
+            out_dram,
+            slice(j * HEADS_PER_BANK, (j + 1) * HEADS_PER_BANK),
+            v_rows[:].rearrange("p (h d) -> p h d", d=FEATURES),
+        )
+
+
+def tile_selfattention_pa_k_kernel(
+    tc, x, pe, qkv_w_words, qkv_w_scales, qkv_b, q_scale, k_scale, out_0, out_1, out_2
+):
+    nc = tc.nc
+    with ExitStack() as ctx:
+        keep = ctx.enter_context(tc.tile_pool(name="keep", bufs=1))
+        x_pool = ctx.enter_context(tc.tile_pool(name="x_pool", bufs=X_CHUNKS))
+        grouped_pool = ctx.enter_context(tc.tile_pool(name="grouped_pool", bufs=2))
+        w_pool = ctx.enter_context(tc.tile_pool(name="w_pool", bufs=W_BUFS))
+        work = ctx.enter_context(tc.tile_pool(name="work", bufs=1))
+        psum = ctx.enter_context(tc.psum_pool(name="psum", bufs=8))
+
+        x_chunks = load_x(nc, x_pool, x)
+        w_planes = load_w_scales(nc, keep, qkv_w_scales)
+        x_codes, x_planes = quantise_x(nc, keep, grouped_pool, psum, x_chunks)
+        bias_planes, bias_v, tables = spread_constants(nc, keep, psum, pe, qkv_b, q_scale, k_scale)
+
+        outs = [out_0, out_1, out_2]
+        for stream in range(STREAMS):
+            acc = project(nc, w_pool, psum, qkv_w_words, w_planes, x_codes, x_planes, stream)
+            if stream < 2:
+                norm_and_rotate(nc, work, acc, bias_planes[:, stream], tables[:, stream], outs[stream])
+            else:
+                add_bias_to_v(nc, work, acc, bias_v, outs[stream])

@@ -63,18 +63,16 @@ def load_w_scales(nc, keep, qkv_w_scales):
     nc.vector.memset(w_planes[:].bitcast(I32), 0)
     for j in range(GROUPS // PLANES_PER_TILE):
         for quadrant in range(4):
-            nc.sync.dma_start(
-                out=w_planes[32 * quadrant : 32 * quadrant + 16, j, :].bitcast(I32),
+            nc.gpsimd.dma_start(
+                out=w_planes[32 * quadrant : 32 * quadrant + 16, j, :].bitcast(F32),
                 in_=qkv_w_scales[
                     PLANES_PER_TILE * j : PLANES_PER_TILE * (j + 1), 4 * quadrant : 4 * quadrant + 4, :
-                ].bitcast(I32),
+                ].bitcast(F32),
             )
     return w_planes
 
 
-def quantise_x(nc, keep, grouped_pool, psum, x_chunks):
-    ident = keep.tile([P, P], F32)
-    make_identity(nc, ident[:])
+def quantise_x(nc, keep, grouped_pool, psum, ident, x_chunks):
     x_codes = keep.tile([P, GROUPS, P], U32, align_bytes=64)
     x_planes = keep.tile([P, GROUPS, P], U8, align_bytes=64)
     for c in range(X_CHUNKS):
@@ -264,9 +262,11 @@ def tile_selfattention_pa_k_kernel(
         work = ctx.enter_context(tc.tile_pool(name="work", bufs=1))
         psum = ctx.enter_context(tc.psum_pool(name="psum", bufs=8))
 
+        ident = keep.tile([P, P], F32)
+        make_identity(nc, ident[:])
         x_chunks = load_x(nc, x_pool, x)
         w_planes = load_w_scales(nc, keep, qkv_w_scales)
-        x_codes, x_planes = quantise_x(nc, keep, grouped_pool, psum, x_chunks)
+        x_codes, x_planes = quantise_x(nc, keep, grouped_pool, psum, ident, x_chunks)
         bias_planes, bias_v, tables = spread_constants(nc, keep, psum, pe, qkv_b, q_scale, k_scale)
 
         outs = [out_0, out_1, out_2]

@@ -28,24 +28,42 @@ K_ALL = 8192
 GROUPS = K_ALL // K_GROUP
 WORDS_PER_GROUP = K_GROUP // 2
 
-STREAMS = 3
 STREAM_COLS = HEADS * FEATURES
-N_ALL = STREAMS * STREAM_COLS
+QK_COLS = 2 * STREAM_COLS
+N_ALL = 3 * STREAM_COLS
 BANK = 512
 BANKS_PER_STREAM = STREAM_COLS // BANK
 HEADS_PER_BANK = BANK // FEATURES
+PSUM_BANKS = 8
 
 X_CHUNKS = 4
 CHUNK_GROUPS = GROUPS // X_CHUNKS
 CHUNK_K = K_ALL // X_CHUNKS
 
 PLANES_PER_TILE = 4
-W_GROUPS_PER_LOAD = 2
-W_BUFS = 12
+QK_BUFS = 8
+V_BUFS = 12
 
 ROW_COLS = N_ALL + BANK
 
 FLOPS = 2 * P * K_ALL * N_ALL
+
+
+def load_small_inputs(nc, keep, pe, qkv_b, q_scale, k_scale):
+    row = keep.tile([P, ROW_COLS], BF16)
+    nc.vector.memset(row[:], 0.0)
+    nc.scalar.dma_start(out=row[0:1, 0:N_ALL], in_=qkv_b.rearrange("(o n) -> o n", o=1))
+    nc.scalar.dma_start(out=row[0:1, N_ALL : N_ALL + FEATURES], in_=q_scale.rearrange("(o n) -> o n", o=1))
+    nc.scalar.dma_start(
+        out=row[0:1, N_ALL + FEATURES : N_ALL + 2 * FEATURES], in_=k_scale.rearrange("(o n) -> o n", o=1)
+    )
+    pe_sb = keep.tile([P, PAIRS * 4], BF16)
+    for b in range(BATCHES):
+        nc.scalar.dma_start(
+            out=pe_sb[b * POSITIONS : (b + 1) * POSITIONS, :],
+            in_=pe.rearrange("a b l i r c -> (a b l) (i r c)"),
+        )
+    return row, pe_sb
 
 
 def load_x(nc, x_pool, x):
@@ -58,18 +76,15 @@ def load_x(nc, x_pool, x):
     return x_chunks
 
 
-def load_w_scales(nc, keep, qkv_w_scales):
-    w_planes = keep.tile([P, GROUPS // PLANES_PER_TILE, N_ALL], U8, align_bytes=64)
-    nc.vector.memset(w_planes[:].bitcast(I32), 0)
+def load_w_scales(nc, w_planes, qkv_w_scales):
     for j in range(GROUPS // PLANES_PER_TILE):
         for quadrant in range(4):
-            nc.gpsimd.dma_start(
-                out=w_planes[32 * quadrant : 32 * quadrant + 16, j, :].bitcast(F32),
+            nc.sync.dma_start(
+                out=w_planes[32 * quadrant : 32 * quadrant + 16, j, :].bitcast(I32),
                 in_=qkv_w_scales[
                     PLANES_PER_TILE * j : PLANES_PER_TILE * (j + 1), 4 * quadrant : 4 * quadrant + 4, :
-                ].bitcast(F32),
+                ].bitcast(I32),
             )
-    return w_planes
 
 
 def quantise_x(nc, keep, grouped_pool, psum, ident, x_chunks):
@@ -101,23 +116,9 @@ def quantise_x(nc, keep, grouped_pool, psum, ident, x_chunks):
     return x_codes, x_planes
 
 
-def spread_constants(nc, keep, psum, pe, qkv_b, q_scale, k_scale):
-    row = keep.tile([P, ROW_COLS], BF16)
-    nc.vector.memset(row[:], 0.0)
+def spread_constants(nc, keep, psum, row, pe_sb):
     ones = keep.tile([P, P], BF16)
     nc.vector.memset(ones[:], 1.0)
-    nc.scalar.dma_start(out=row[0:1, 0:N_ALL], in_=qkv_b.rearrange("(o n) -> o n", o=1))
-    nc.scalar.dma_start(out=row[0:1, N_ALL : N_ALL + FEATURES], in_=q_scale.rearrange("(o n) -> o n", o=1))
-    nc.scalar.dma_start(
-        out=row[0:1, N_ALL + FEATURES : N_ALL + 2 * FEATURES], in_=k_scale.rearrange("(o n) -> o n", o=1)
-    )
-    pe_sb = keep.tile([P, PAIRS * 4], BF16)
-    for b in range(BATCHES):
-        nc.scalar.dma_start(
-            out=pe_sb[b * POSITIONS : (b + 1) * POSITIONS, :],
-            in_=pe.rearrange("a b l i r c -> (a b l) (i r c)"),
-        )
-
     bias_planes = keep.tile([P, 2, 2, HEADS, PAIRS], F32)
     bias_v = keep.tile([P, STREAM_COLS], F32)
     tables = keep.tile([P, 2, 2, 2, PAIRS], F32)
@@ -145,109 +146,103 @@ def spread_constants(nc, keep, psum, pe, qkv_b, q_scale, k_scale):
     return bias_planes, bias_v, tables
 
 
-def project(nc, w_pool, psum, qkv_w_words, w_planes, x_codes, x_planes, stream):
-    first_col = stream * STREAM_COLS
-    w_rows = qkv_w_words.rearrange("g p n t -> p g (n t)")
+def project(nc, w_pool, psum, qkv_w_words, w_planes, x_codes, x_planes, first_col, n_cols):
     acc = []
-    for j in range(BANKS_PER_STREAM):
+    for j in range(n_cols // BANK):
         bank = psum.tile([P, BANK], F32, tag="bank")
         acc.append(bank)
-    for load in range(GROUPS // W_GROUPS_PER_LOAD):
-        first_group = load * W_GROUPS_PER_LOAD
-        w_words = w_pool.tile([P, W_GROUPS_PER_LOAD, STREAM_COLS], U32, align_bytes=64)
+    for g in range(GROUPS):
+        w_words = w_pool.tile([P, n_cols], U32, align_bytes=64)
         nc.sync.dma_start(
             out=w_words[:].bitcast(I32),
-            in_=w_rows[
-                :, first_group : first_group + W_GROUPS_PER_LOAD, PACK * first_col : PACK * (first_col + STREAM_COLS)
-            ].bitcast(I32),
+            in_=qkv_w_words[g]
+            .rearrange("p n t -> p (n t)")[:, PACK * first_col : PACK * (first_col + n_cols)]
+            .bitcast(I32),
         )
-        for j in range(BANKS_PER_STREAM):
-            for gl in range(W_GROUPS_PER_LOAD):
-                g = first_group + gl
-                plane_start = 4 * (g % PLANES_PER_TILE)
-                nc.tensor.matmul_mx(
-                    out=acc[j][:],
-                    lhsT=x_codes[:, g, :].bitcast(FP8X4),
-                    lhsT_scale=x_planes[:, g, :],
-                    rhs=w_words[:, gl, j * BANK : (j + 1) * BANK].bitcast(FP8X4),
-                    rhs_scale=w_planes[
-                        plane_start:P, g // PLANES_PER_TILE, first_col + j * BANK : first_col + (j + 1) * BANK
-                    ],
-                    start=(g == 0),
-                    stop=(g == GROUPS - 1),
-                )
+        plane_start = 4 * (g % PLANES_PER_TILE)
+        for j in range(n_cols // BANK):
+            nc.tensor.matmul_mx(
+                out=acc[j][:],
+                lhsT=x_codes[:, g, :].bitcast(FP8X4),
+                lhsT_scale=x_planes[:, g, :],
+                rhs=w_words[:, j * BANK : (j + 1) * BANK].bitcast(FP8X4),
+                rhs_scale=w_planes[
+                    plane_start:P, g // PLANES_PER_TILE, first_col + j * BANK : first_col + (j + 1) * BANK
+                ],
+                start=(g == 0),
+                stop=(g == GROUPS - 1),
+            )
     return acc
 
 
 def store_heads(nc, out_dram, heads, rows):
     for b in range(BATCHES):
-        nc.scalar.dma_start(
+        nc.sync.dma_start(
             out=out_dram[b, heads].rearrange("h l d -> l h d"),
             in_=rows[b * POSITIONS : (b + 1) * POSITIONS],
         )
 
 
-def norm_and_rotate(nc, work, acc, bias_planes, table, out_dram):
+def norm_and_rotate(nc, work, acc_qk, bias_planes, tables):
     planes_shape = [P, 2, HEADS, PAIRS]
-    biased = work.tile(planes_shape, F32)
-    for j in range(BANKS_PER_STREAM):
-        heads = slice(j * HEADS_PER_BANK, (j + 1) * HEADS_PER_BANK)
+    biased = []
+    for s in range(2):
+        with_bias = work.tile(planes_shape, F32, name="biased%d" % s)
+        for j in range(BANKS_PER_STREAM):
+            heads = slice(j * HEADS_PER_BANK, (j + 1) * HEADS_PER_BANK)
+            nc.vector.tensor_tensor(
+                out=with_bias[:, :, heads, :],
+                in0=acc_qk[s * BANKS_PER_STREAM + j][:].rearrange("p (h i e) -> p e h i", i=PAIRS, e=2),
+                in1=bias_planes[:, s, :, heads, :],
+                op=ADD,
+            )
+        biased.append(with_bias)
+
+    sums = work.tile([P, 2, HEADS], F32)
+    for s in range(2):
+        squares = work.tile(planes_shape, F32)
+        for h in range(HEADS):
+            nc.scalar.activation(
+                out=squares[:, :, h, :], in_=biased[s][:, :, h, :], func=SQUARE, accum_out=sums[:, s, h : h + 1]
+            )
+
+    rotated = []
+    for s in range(2):
+        from_plane = []
+        for c in range(2):
+            part = work.tile(planes_shape, F32, name="from_plane%d" % c)
+            nc.vector.tensor_tensor(
+                out=part[:],
+                in0=biased[s][:, c].unsqueeze(1).to_broadcast(planes_shape),
+                in1=tables[:, s, c].unsqueeze(2).to_broadcast(planes_shape),
+                op=MULT,
+            )
+            from_plane.append(part)
+        mixed = work.tile([P, HEADS, PAIRS, 2], F32, name="rotated%d" % s)
         nc.vector.tensor_tensor(
-            out=biased[:, :, heads, :],
-            in0=acc[j][:].rearrange("p (h i e) -> p e h i", i=PAIRS, e=2),
-            in1=bias_planes[:, :, heads, :],
+            out=mixed[:],
+            in0=from_plane[0][:].rearrange("p r h i -> p h i r"),
+            in1=from_plane[1][:].rearrange("p r h i -> p h i r"),
             op=ADD,
         )
+        rotated.append(mixed[:].rearrange("p h i r -> p h (i r)"))
 
-    squares = work.tile(planes_shape, F32)
-    nc.scalar.activation(out=squares[:], in_=biased[:], func=SQUARE)
-    sums = work.tile([P, HEADS], F32)
-    nc.vector.tensor_reduce(
-        out=sums[:], in_=squares[:].rearrange("p e h i -> p h e i"), axis=mybir.AxisListType.XY, op=ADD
-    )
-    mean_eps = work.tile([P, HEADS], F32)
+    mean_eps = work.tile([P, 2, HEADS], F32)
     nc.vector.tensor_scalar(
         out=mean_eps[:], in0=sums[:], scalar1=1.0 / FEATURES, scalar2=EPS, op0=MULT, op1=ADD
     )
-    rms = work.tile([P, HEADS], F32)
+    rms = work.tile([P, 2, HEADS], F32)
     nc.scalar.activation(out=rms[:], in_=mean_eps[:], func=SQRT)
-    rrms = work.tile([P, HEADS], F32)
+    rrms = work.tile([P, 2, HEADS], F32)
     nc.vector.reciprocal(out=rrms[:], in_=rms[:])
-
-    normed = work.tile(planes_shape, F32)
-    nc.vector.tensor_tensor(
-        out=normed[:], in0=biased[:], in1=rrms[:].unsqueeze(1).unsqueeze(3).to_broadcast(planes_shape), op=MULT
-    )
-    from_plane = []
-    for c in range(2):
-        part = work.tile(planes_shape, F32, name="from_plane%d" % c)
+    for s in range(2):
         nc.vector.tensor_tensor(
-            out=part[:],
-            in0=normed[:, c].unsqueeze(1).to_broadcast(planes_shape),
-            in1=table[:, c].unsqueeze(2).to_broadcast(planes_shape),
+            out=rotated[s],
+            in0=rotated[s],
+            in1=rrms[:, s].unsqueeze(2).to_broadcast([P, HEADS, FEATURES]),
             op=MULT,
         )
-        from_plane.append(part)
-    rotated = work.tile([P, HEADS, PAIRS, 2], F32)
-    nc.vector.tensor_tensor(
-        out=rotated[:],
-        in0=from_plane[0][:].rearrange("p r h i -> p h i r"),
-        in1=from_plane[1][:].rearrange("p r h i -> p h i r"),
-        op=ADD,
-    )
-    store_heads(nc, out_dram, slice(0, HEADS), rotated[:].rearrange("p h i r -> p h (i r)"))
-
-
-def add_bias_to_v(nc, work, acc, bias_v, out_dram):
-    for j in range(BANKS_PER_STREAM):
-        v_rows = work.tile([P, BANK], F32, name="v_rows%d" % j)
-        nc.vector.tensor_tensor(out=v_rows[:], in0=acc[j][:], in1=bias_v[:, j * BANK : (j + 1) * BANK], op=ADD)
-        store_heads(
-            nc,
-            out_dram,
-            slice(j * HEADS_PER_BANK, (j + 1) * HEADS_PER_BANK),
-            v_rows[:].rearrange("p (h d) -> p h d", d=FEATURES),
-        )
+    return rotated
 
 
 def tile_selfattention_pa_k_kernel(
@@ -255,24 +250,39 @@ def tile_selfattention_pa_k_kernel(
 ):
     nc = tc.nc
     with ExitStack() as ctx:
+        ctx.enter_context(tc.manual_schedule())
         keep = ctx.enter_context(tc.tile_pool(name="keep", bufs=1))
         x_pool = ctx.enter_context(tc.tile_pool(name="x_pool", bufs=X_CHUNKS))
         grouped_pool = ctx.enter_context(tc.tile_pool(name="grouped_pool", bufs=2))
-        w_pool = ctx.enter_context(tc.tile_pool(name="w_pool", bufs=W_BUFS))
+        w_qk_pool = ctx.enter_context(tc.tile_pool(name="w_qk_pool", bufs=QK_BUFS))
+        w_v_pool = ctx.enter_context(tc.tile_pool(name="w_v_pool", bufs=V_BUFS))
         work = ctx.enter_context(tc.tile_pool(name="work", bufs=1))
-        psum = ctx.enter_context(tc.psum_pool(name="psum", bufs=8))
+        psum = ctx.enter_context(tc.psum_pool(name="psum", bufs=PSUM_BANKS))
 
         ident = keep.tile([P, P], F32)
         make_identity(nc, ident[:])
-        x_chunks = load_x(nc, x_pool, x)
-        w_planes = load_w_scales(nc, keep, qkv_w_scales)
-        x_codes, x_planes = quantise_x(nc, keep, grouped_pool, psum, ident, x_chunks)
-        bias_planes, bias_v, tables = spread_constants(nc, keep, psum, pe, qkv_b, q_scale, k_scale)
+        w_planes = keep.tile([P, GROUPS // PLANES_PER_TILE, N_ALL], U8, align_bytes=64)
+        nc.vector.memset(w_planes[:].bitcast(I32), 0)
+        row, pe_sb = load_small_inputs(nc, keep, pe, qkv_b, q_scale, k_scale)
 
-        outs = [out_0, out_1, out_2]
-        for stream in range(STREAMS):
-            acc = project(nc, w_pool, psum, qkv_w_words, w_planes, x_codes, x_planes, stream)
-            if stream < 2:
-                norm_and_rotate(nc, work, acc, bias_planes[:, stream], tables[:, stream], outs[stream])
-            else:
-                add_bias_to_v(nc, work, acc, bias_v, outs[stream])
+        x_chunks = load_x(nc, x_pool, x)
+        load_w_scales(nc, w_planes, qkv_w_scales)
+        x_codes, x_planes = quantise_x(nc, keep, grouped_pool, psum, ident, x_chunks)
+        bias_planes, bias_v, tables = spread_constants(nc, keep, psum, row, pe_sb)
+
+        acc_qk = project(nc, w_qk_pool, psum, qkv_w_words, w_planes, x_codes, x_planes, 0, QK_COLS)
+        acc_v = project(nc, w_v_pool, psum, qkv_w_words, w_planes, x_codes, x_planes, QK_COLS, STREAM_COLS)
+
+        rotated = norm_and_rotate(nc, work, acc_qk, bias_planes, tables)
+        store_heads(nc, out_0, slice(0, HEADS), rotated[0])
+        store_heads(nc, out_1, slice(0, HEADS), rotated[1])
+
+        for j in range(BANKS_PER_STREAM):
+            v_rows = work.tile([P, BANK], F32, name="v_rows%d" % j)
+            nc.vector.tensor_tensor(out=v_rows[:], in0=acc_v[j][:], in1=bias_v[:, j * BANK : (j + 1) * BANK], op=ADD)
+            store_heads(
+                nc,
+                out_2,
+                slice(j * HEADS_PER_BANK, (j + 1) * HEADS_PER_BANK),
+                v_rows[:].rearrange("p (h d) -> p h d", d=FEATURES),
+            )

@@ -51,7 +51,7 @@ FLOPS = 2 * P * K_ALL * N_ALL
 
 def load_small_inputs(nc, keep, pe, qkv_b, q_scale, k_scale):
     row = keep.tile([P, ROW_COLS], BF16)
-    nc.vector.memset(row[:], 0.0)
+    nc.vector.memset(row[:].bitcast(I32), 0)
     nc.scalar.dma_start(out=row[0:1, 0:N_ALL], in_=qkv_b.rearrange("(o n) -> o n", o=1))
     nc.scalar.dma_start(out=row[0:1, N_ALL : N_ALL + FEATURES], in_=q_scale.rearrange("(o n) -> o n", o=1))
     nc.scalar.dma_start(
@@ -79,11 +79,11 @@ def load_x(nc, x_pool, x):
 def load_w_scales(nc, w_planes, qkv_w_scales):
     for j in range(GROUPS // PLANES_PER_TILE):
         for quadrant in range(4):
-            nc.sync.dma_start(
-                out=w_planes[32 * quadrant : 32 * quadrant + 16, j, :].bitcast(I32),
+            nc.gpsimd.dma_start(
+                out=w_planes[32 * quadrant : 32 * quadrant + 16, j, :].bitcast(F32),
                 in_=qkv_w_scales[
                     PLANES_PER_TILE * j : PLANES_PER_TILE * (j + 1), 4 * quadrant : 4 * quadrant + 4, :
-                ].bitcast(I32),
+                ].bitcast(F32),
             )
 
 
@@ -262,8 +262,10 @@ def tile_selfattention_pa_k_kernel(
         ident = keep.tile([P, P], F32)
         make_identity(nc, ident[:])
         w_planes = keep.tile([P, GROUPS // PLANES_PER_TILE, N_ALL], U8, align_bytes=64)
-        nc.vector.memset(w_planes[:].bitcast(I32), 0)
+        nc.vector.memset(w_planes[:, 0, :].bitcast(I32), 0)
         row, pe_sb = load_small_inputs(nc, keep, pe, qkv_b, q_scale, k_scale)
+        for j in range(1, GROUPS // PLANES_PER_TILE):
+            nc.vector.memset(w_planes[:, j, :].bitcast(I32), 0)
 
         x_chunks = load_x(nc, x_pool, x)
         load_w_scales(nc, w_planes, qkv_w_scales)

@@ -60,18 +60,18 @@ def load_small_inputs(nc, keep, pe, qkv_b, q_scale, k_scale):
     pe_sb = keep.tile([P, PAIRS * 4], BF16)
     for b in range(BATCHES):
         nc.scalar.dma_start(
-            out=pe_sb[b * POSITIONS : (b + 1) * POSITIONS, :],
+            out=pe_sb[b:P:BATCHES, :],
             in_=pe.rearrange("a b l i r c -> (a b l) (i r c)"),
         )
     return row, pe_sb
 
 
 def load_x(nc, x_pool, x):
-    x_rows = x.rearrange("b l k -> (b l) k")
     x_chunks = []
     for c in range(X_CHUNKS):
         x_chunk = x_pool.tile([P, CHUNK_K], BF16)
-        nc.sync.dma_start(out=x_chunk[:], in_=x_rows[:, c * CHUNK_K : (c + 1) * CHUNK_K])
+        for b in range(BATCHES):
+            nc.sync.dma_start(out=x_chunk[b:P:BATCHES, :], in_=x[b, :, c * CHUNK_K : (c + 1) * CHUNK_K])
         x_chunks.append(x_chunk)
     return x_chunks
 
@@ -179,7 +179,7 @@ def store_heads(nc, out_dram, heads, rows):
     for b in range(BATCHES):
         nc.sync.dma_start(
             out=out_dram[b, heads].rearrange("h l d -> l h d"),
-            in_=rows[b * POSITIONS : (b + 1) * POSITIONS],
+            in_=rows[b:P:BATCHES],
         )
 
 

@@ -39,6 +39,11 @@ PSUM_BANKS = 8
 X_CHUNKS = 4
 CHUNK_GROUPS = GROUPS // X_CHUNKS
 CHUNK_K = K_ALL // X_CHUNKS
+X_LOADS = 2
+X_LOAD_K = K_ALL // X_LOADS
+
+RUN = 8
+Q_TURN_1, Q_TURN_2, K_TURN_1, K_TURN_2 = 6, 8, 10, 12
 
 PLANES_PER_TILE = 4
 QK_BUFS = 8
@@ -68,11 +73,12 @@ def load_small_inputs(nc, keep, pe, qkv_b, q_scale, k_scale):
 
 def load_x(nc, x_pool, x):
     x_chunks = []
-    for c in range(X_CHUNKS):
-        x_chunk = x_pool.tile([P, CHUNK_K], BF16)
+    for c in range(X_LOADS):
+        x_half = x_pool.tile([P, X_LOAD_K], BF16)
         for b in range(BATCHES):
-            nc.sync.dma_start(out=x_chunk[b:P:BATCHES, :], in_=x[b, :, c * CHUNK_K : (c + 1) * CHUNK_K])
-        x_chunks.append(x_chunk)
+            nc.sync.dma_start(out=x_half[b:P:BATCHES, :], in_=x[b, :, c * X_LOAD_K : (c + 1) * X_LOAD_K])
+        for i in range(X_LOAD_K // CHUNK_K):
+            x_chunks.append(x_half[:, i * CHUNK_K : (i + 1) * CHUNK_K])
     return x_chunks
 
 
@@ -91,7 +97,7 @@ def quantise_x(nc, keep, grouped_pool, psum, ident, x_chunks):
     x_codes = keep.tile([P, GROUPS, P], U32, align_bytes=64)
     x_planes = keep.tile([P, GROUPS, P], U8, align_bytes=64)
     for c in range(X_CHUNKS):
-        x_words = x_chunks[c][:].bitcast(F32)
+        x_words = x_chunks[c].bitcast(F32)
         grouped = grouped_pool.tile([P, CHUNK_GROUPS, P, PACK], BF16, align_bytes=64)
         grouped_words = grouped[:].bitcast(F32)
         for half in range(2):
@@ -146,33 +152,36 @@ def spread_constants(nc, keep, psum, row, pe_sb):
     return bias_planes, bias_v, tables
 
 
-def project(nc, w_pool, psum, qkv_w_words, w_planes, x_codes, x_planes, first_col, n_cols):
+def open_banks(pool, n_cols):
     acc = []
     for j in range(n_cols // BANK):
-        bank = psum.tile([P, BANK], F32, tag="bank")
+        bank = pool.tile([P, BANK], F32, tag="bank")
         acc.append(bank)
-    for g in range(GROUPS):
-        w_words = w_pool.tile([P, n_cols], U32, align_bytes=64)
-        nc.sync.dma_start(
-            out=w_words[:].bitcast(I32),
-            in_=qkv_w_words[g]
-            .rearrange("p n t -> p (n t)")[:, PACK * first_col : PACK * (first_col + n_cols)]
-            .bitcast(I32),
-        )
-        plane_start = 4 * (g % PLANES_PER_TILE)
-        for j in range(n_cols // BANK):
-            nc.tensor.matmul_mx(
-                out=acc[j][:],
-                lhsT=x_codes[:, g, :].bitcast(FP8X4),
-                lhsT_scale=x_planes[:, g, :],
-                rhs=w_words[:, j * BANK : (j + 1) * BANK].bitcast(FP8X4),
-                rhs_scale=w_planes[
-                    plane_start:P, g // PLANES_PER_TILE, first_col + j * BANK : first_col + (j + 1) * BANK
-                ],
-                start=(g == 0),
-                stop=(g == GROUPS - 1),
-            )
     return acc
+
+
+def multiply_group(nc, w_pool, acc, qkv_w_words, w_planes, x_codes, x_planes, first_col, g):
+    n_cols = len(acc) * BANK
+    w_words = w_pool.tile([P, n_cols], U32, align_bytes=64)
+    nc.sync.dma_start(
+        out=w_words[:].bitcast(I32),
+        in_=qkv_w_words[g]
+        .rearrange("p n t -> p (n t)")[:, PACK * first_col : PACK * (first_col + n_cols)]
+        .bitcast(I32),
+    )
+    plane_start = 4 * (g % PLANES_PER_TILE)
+    for j in range(n_cols // BANK):
+        nc.tensor.matmul_mx(
+            out=acc[j][:],
+            lhsT=x_codes[:, g, :].bitcast(FP8X4),
+            lhsT_scale=x_planes[:, g, :],
+            rhs=w_words[:, j * BANK : (j + 1) * BANK].bitcast(FP8X4),
+            rhs_scale=w_planes[
+                plane_start:P, g // PLANES_PER_TILE, first_col + j * BANK : first_col + (j + 1) * BANK
+            ],
+            start=(g == 0),
+            stop=(g == GROUPS - 1),
+        )
 
 
 def store_heads(nc, out_dram, heads, rows):
@@ -191,7 +200,7 @@ def norm_and_rotate(nc, work, acc_qk, bias_planes, tables):
         for j in range(BANKS_PER_STREAM):
             heads = slice(j * HEADS_PER_BANK, (j + 1) * HEADS_PER_BANK)
             nc.vector.tensor_tensor(
-                out=with_bias[:, :, heads, :],
+                out=with_bias[:].rearrange("p e (c a) i -> p e c a i", a=2)[:, :, :, j, :],
                 in0=acc_qk[s * BANKS_PER_STREAM + j][:].rearrange("p (h i e) -> p e h i", i=PAIRS, e=2),
                 in1=bias_planes[:, s, :, heads, :],
                 op=ADD,
@@ -206,43 +215,80 @@ def norm_and_rotate(nc, work, acc_qk, bias_planes, tables):
                 out=squares[:, :, h, :], in_=biased[s][:, :, h, :], func=SQUARE, accum_out=sums[:, s, h : h + 1]
             )
 
-    rotated = []
-    for s in range(2):
-        from_plane = []
-        for c in range(2):
-            part = work.tile(planes_shape, F32, name="from_plane%d" % c)
-            nc.vector.tensor_tensor(
-                out=part[:],
-                in0=biased[s][:, c].unsqueeze(1).to_broadcast(planes_shape),
-                in1=tables[:, s, c].unsqueeze(2).to_broadcast(planes_shape),
-                op=MULT,
-            )
-            from_plane.append(part)
+    def products(s, c):
+        part = work.tile(planes_shape, F32, name="from_plane%d" % c)
+        nc.vector.tensor_tensor(
+            out=part[:],
+            in0=biased[s][:, c].unsqueeze(1).to_broadcast(planes_shape),
+            in1=tables[:, s, c].unsqueeze(2).to_broadcast(planes_shape),
+            op=MULT,
+        )
+        return part
+
+    def mix(s, part0, part1):
         mixed = work.tile([P, HEADS, PAIRS, 2], F32, name="rotated%d" % s)
         nc.vector.tensor_tensor(
             out=mixed[:],
-            in0=from_plane[0][:].rearrange("p r h i -> p h i r"),
-            in1=from_plane[1][:].rearrange("p r h i -> p h i r"),
+            in0=part0[:].rearrange("p r h i -> p h i r"),
+            in1=part1[:].rearrange("p r h i -> p h i r"),
             op=ADD,
         )
-        rotated.append(mixed[:].rearrange("p h i r -> p h (i r)"))
+        return mixed[:].rearrange("p h i r -> p h (i r)")
 
+    def normalise(s, rows):
+        nc.vector.tensor_tensor(
+            out=rows, in0=rows, in1=rrms[:, s].unsqueeze(2).to_broadcast([P, HEADS, FEATURES]), op=MULT
+        )
+
+    q_rows = mix(0, products(0, 0), products(0, 1))
     mean_eps = work.tile([P, 2, HEADS], F32)
     nc.vector.tensor_scalar(
         out=mean_eps[:], in0=sums[:], scalar1=1.0 / FEATURES, scalar2=EPS, op0=MULT, op1=ADD
     )
     rms = work.tile([P, 2, HEADS], F32)
     nc.scalar.activation(out=rms[:], in_=mean_eps[:], func=SQRT)
+    k_part = products(1, 0)
     rrms = work.tile([P, 2, HEADS], F32)
     nc.vector.reciprocal(out=rrms[:], in_=rms[:])
-    for s in range(2):
-        nc.vector.tensor_tensor(
-            out=rotated[s],
-            in0=rotated[s],
-            in1=rrms[:, s].unsqueeze(2).to_broadcast([P, HEADS, FEATURES]),
-            op=MULT,
+    normalise(0, q_rows)
+    k_rows = mix(1, k_part, products(1, 1))
+    normalise(1, k_rows)
+    return q_rows, k_rows
+
+
+def features_to_partitions(nc, work, psum, ident, rows, s):
+    flat = rows.rearrange("p h d -> p (h d)")
+    columns = work.tile([P, RUN, P], F32, name="columns%d" % s)
+    for half in range(2):
+        bank = psum.tile([P, 4, P], F32, tag="bank")
+        for i in range(4):
+            c = 4 * half + i
+            nc.tensor.transpose(bank[:, i, :], flat[:, c * P : (c + 1) * P], ident[:])
+        nc.scalar.copy(
+            out=columns[:, :, half * 64 : (half + 1) * 64].rearrange("p t (q b) -> p t q b", b=BATCHES),
+            in_=bank[:].rearrange("p c (m t b) -> p t (c m) b", t=RUN, b=BATCHES),
         )
-    return rotated
+    return columns
+
+
+def positions_to_partitions(nc, work, psum, ident, columns, s):
+    runs = work.tile([P, 2, RUN, FEATURES], F32, name="runs%d" % s)
+    for half in range(2):
+        bank = psum.tile([P, 4, P], F32, tag="bank")
+        for i in range(4):
+            nc.tensor.transpose(bank[:, i, :], columns[:, 4 * half + i, :], ident[:])
+        nc.scalar.copy(
+            out=runs[:, :, 4 * half : 4 * half + 4, :], in_=bank[:].rearrange("p t (a d) -> p a t d", a=2)
+        )
+    return runs
+
+
+def store_runs(nc, out_dram, runs):
+    for b in range(BATCHES):
+        nc.sync.dma_start(
+            out=out_dram[b].rearrange("(a c) (m t) d -> (c m) a (t d)", a=2, t=RUN),
+            in_=runs[b:P:BATCHES].rearrange("p a t d -> p a (t d)"),
+        )
 
 
 def tile_selfattention_pa_k_kernel(
@@ -252,32 +298,45 @@ def tile_selfattention_pa_k_kernel(
     with ExitStack() as ctx:
         ctx.enter_context(tc.manual_schedule())
         keep = ctx.enter_context(tc.tile_pool(name="keep", bufs=1))
-        x_pool = ctx.enter_context(tc.tile_pool(name="x_pool", bufs=X_CHUNKS))
+        x_pool = ctx.enter_context(tc.tile_pool(name="x_pool", bufs=X_LOADS))
         grouped_pool = ctx.enter_context(tc.tile_pool(name="grouped_pool", bufs=2))
         w_qk_pool = ctx.enter_context(tc.tile_pool(name="w_qk_pool", bufs=QK_BUFS))
         w_v_pool = ctx.enter_context(tc.tile_pool(name="w_v_pool", bufs=V_BUFS))
         work = ctx.enter_context(tc.tile_pool(name="work", bufs=1))
-        psum = ctx.enter_context(tc.psum_pool(name="psum", bufs=PSUM_BANKS))
+        psum = ctx.enter_context(tc.psum_pool(name="psum", bufs=PSUM_BANKS - BANKS_PER_STREAM))
+        psum_v = ctx.enter_context(tc.psum_pool(name="psum_v", bufs=BANKS_PER_STREAM))
 
         ident = keep.tile([P, P], F32)
         make_identity(nc, ident[:])
         w_planes = keep.tile([P, GROUPS // PLANES_PER_TILE, N_ALL], U8, align_bytes=64)
         nc.vector.memset(w_planes[:, 0, :].bitcast(I32), 0)
+        x_chunks = load_x(nc, x_pool, x)
         row, pe_sb = load_small_inputs(nc, keep, pe, qkv_b, q_scale, k_scale)
         for j in range(1, GROUPS // PLANES_PER_TILE):
             nc.vector.memset(w_planes[:, j, :].bitcast(I32), 0)
 
-        x_chunks = load_x(nc, x_pool, x)
         load_w_scales(nc, w_planes, qkv_w_scales)
         x_codes, x_planes = quantise_x(nc, keep, grouped_pool, psum, ident, x_chunks)
         bias_planes, bias_v, tables = spread_constants(nc, keep, psum, row, pe_sb)
 
-        acc_qk = project(nc, w_qk_pool, psum, qkv_w_words, w_planes, x_codes, x_planes, 0, QK_COLS)
-        acc_v = project(nc, w_v_pool, psum, qkv_w_words, w_planes, x_codes, x_planes, QK_COLS, STREAM_COLS)
+        acc_qk = open_banks(psum, QK_COLS)
+        for g in range(GROUPS):
+            multiply_group(nc, w_qk_pool, acc_qk, qkv_w_words, w_planes, x_codes, x_planes, 0, g)
+        q_rows, k_rows = norm_and_rotate(nc, work, acc_qk, bias_planes, tables)
 
-        rotated = norm_and_rotate(nc, work, acc_qk, bias_planes, tables)
-        store_heads(nc, out_0, slice(0, HEADS), rotated[0])
-        store_heads(nc, out_1, slice(0, HEADS), rotated[1])
+        acc_v = open_banks(psum_v, STREAM_COLS)
+        for g in range(GROUPS):
+            multiply_group(nc, w_v_pool, acc_v, qkv_w_words, w_planes, x_codes, x_planes, QK_COLS, g)
+            if g == Q_TURN_1:
+                q_columns = features_to_partitions(nc, work, psum, ident, q_rows, 0)
+            elif g == Q_TURN_2:
+                q_runs = positions_to_partitions(nc, work, psum, ident, q_columns, 0)
+            elif g == K_TURN_1:
+                k_columns = features_to_partitions(nc, work, psum, ident, k_rows, 1)
+            elif g == K_TURN_2:
+                k_runs = positions_to_partitions(nc, work, psum, ident, k_columns, 1)
+        store_runs(nc, out_0, q_runs)
+        store_runs(nc, out_1, k_runs)
 
         for j in range(BANKS_PER_STREAM):
             v_rows = work.tile([P, BANK], F32, name="v_rows%d" % j)

@@ -43,7 +43,8 @@ X_LOADS = 2
 X_LOAD_K = K_ALL // X_LOADS
 
 RUN = 8
-Q_TURN_1, Q_TURN_2, K_TURN_1, K_TURN_2 = 6, 8, 10, 12
+Q_TURN_1, Q_TURN_2, K_TURN_1, K_TURN_2 = 6, 8, 10, 11
+SPLIT_GROUPS = 4
 
 PLANES_PER_TILE = 4
 QK_BUFS = 8
@@ -325,7 +326,7 @@ def tile_selfattention_pa_k_kernel(
         q_rows, k_rows = norm_and_rotate(nc, work, acc_qk, bias_planes, tables)
 
         acc_v = open_banks(psum_v, STREAM_COLS)
-        for g in range(GROUPS):
+        for g in range(GROUPS - SPLIT_GROUPS):
             multiply_group(nc, w_v_pool, acc_v, qkv_w_words, w_planes, x_codes, x_planes, QK_COLS, g)
             if g == Q_TURN_1:
                 q_columns = features_to_partitions(nc, work, psum, ident, q_rows, 0)
@@ -335,6 +336,12 @@ def tile_selfattention_pa_k_kernel(
                 k_columns = features_to_partitions(nc, work, psum, ident, k_rows, 1)
             elif g == K_TURN_2:
                 k_runs = positions_to_partitions(nc, work, psum, ident, k_columns, 1)
+        for j in range(BANKS_PER_STREAM):
+            for g in range(GROUPS - SPLIT_GROUPS, GROUPS):
+                first_col = QK_COLS + j * BANK
+                multiply_group(
+                    nc, w_v_pool, acc_v[j : j + 1], qkv_w_words, w_planes, x_codes, x_planes, first_col, g
+                )
         store_runs(nc, out_0, q_runs)
         store_runs(nc, out_1, k_runs)
 

@@ -43,7 +43,7 @@ X_LOADS = 2
 X_LOAD_K = K_ALL // X_LOADS
 
 RUN = 8
-Q_TURN_1, Q_TURN_2, K_TURN_1, K_TURN_2 = 6, 8, 10, 11
+Q_TURN_1, Q_TURN_2, K_TURN_1, K_TURN_2 = 2, 8, 7, 9
 SPLIT_GROUPS = 4
 
 PLANES_PER_TILE = 4
@@ -193,68 +193,56 @@ def store_heads(nc, out_dram, heads, rows):
         )
 
 
-def norm_and_rotate(nc, work, acc_qk, bias_planes, tables):
+def norm_and_rotate(nc, work, acc, bias_planes, tables, s):
     planes_shape = [P, 2, HEADS, PAIRS]
-    biased = []
-    for s in range(2):
-        with_bias = work.tile(planes_shape, F32, name="biased%d" % s)
-        for j in range(BANKS_PER_STREAM):
-            heads = slice(j * HEADS_PER_BANK, (j + 1) * HEADS_PER_BANK)
-            nc.vector.tensor_tensor(
-                out=with_bias[:].rearrange("p e (c a) i -> p e c a i", a=2)[:, :, :, j, :],
-                in0=acc_qk[s * BANKS_PER_STREAM + j][:].rearrange("p (h i e) -> p e h i", i=PAIRS, e=2),
-                in1=bias_planes[:, s, :, heads, :],
-                op=ADD,
-            )
-        biased.append(with_bias)
+    biased = work.tile(planes_shape, F32, name="biased%d" % s)
+    for j in range(BANKS_PER_STREAM):
+        heads = slice(j * HEADS_PER_BANK, (j + 1) * HEADS_PER_BANK)
+        nc.vector.tensor_tensor(
+            out=biased[:].rearrange("p e (c a) i -> p e c a i", a=2)[:, :, :, j, :],
+            in0=acc[j][:].rearrange("p (h i e) -> p e h i", i=PAIRS, e=2),
+            in1=bias_planes[:, s, :, heads, :],
+            op=ADD,
+        )
 
-    sums = work.tile([P, 2, HEADS], F32)
-    for s in range(2):
-        squares = work.tile(planes_shape, F32)
-        for h in range(HEADS):
-            nc.scalar.activation(
-                out=squares[:, :, h, :], in_=biased[s][:, :, h, :], func=SQUARE, accum_out=sums[:, s, h : h + 1]
-            )
+    sums = work.tile([P, HEADS], F32, name="sums%d" % s)
+    squares = work.tile(planes_shape, F32)
+    for h in range(HEADS):
+        nc.scalar.activation(
+            out=squares[:, :, h, :], in_=biased[:, :, h, :], func=SQUARE, accum_out=sums[:, h : h + 1]
+        )
 
-    def products(s, c):
+    from_plane = []
+    for c in range(2):
         part = work.tile(planes_shape, F32, name="from_plane%d" % c)
         nc.vector.tensor_tensor(
             out=part[:],
-            in0=biased[s][:, c].unsqueeze(1).to_broadcast(planes_shape),
+            in0=biased[:, c].unsqueeze(1).to_broadcast(planes_shape),
             in1=tables[:, s, c].unsqueeze(2).to_broadcast(planes_shape),
             op=MULT,
         )
-        return part
+        from_plane.append(part)
+    mixed = work.tile([P, HEADS, PAIRS, 2], F32, name="rotated%d" % s)
+    nc.vector.tensor_tensor(
+        out=mixed[:],
+        in0=from_plane[0][:].rearrange("p r h i -> p h i r"),
+        in1=from_plane[1][:].rearrange("p r h i -> p h i r"),
+        op=ADD,
+    )
+    rows = mixed[:].rearrange("p h i r -> p h (i r)")
 
-    def mix(s, part0, part1):
-        mixed = work.tile([P, HEADS, PAIRS, 2], F32, name="rotated%d" % s)
-        nc.vector.tensor_tensor(
-            out=mixed[:],
-            in0=part0[:].rearrange("p r h i -> p h i r"),
-            in1=part1[:].rearrange("p r h i -> p h i r"),
-            op=ADD,
-        )
-        return mixed[:].rearrange("p h i r -> p h (i r)")
-
-    def normalise(s, rows):
-        nc.vector.tensor_tensor(
-            out=rows, in0=rows, in1=rrms[:, s].unsqueeze(2).to_broadcast([P, HEADS, FEATURES]), op=MULT
-        )
-
-    q_rows = mix(0, products(0, 0), products(0, 1))
-    mean_eps = work.tile([P, 2, HEADS], F32)
+    mean_eps = work.tile([P, HEADS], F32, name="mean_eps%d" % s)
     nc.vector.tensor_scalar(
         out=mean_eps[:], in0=sums[:], scalar1=1.0 / FEATURES, scalar2=EPS, op0=MULT, op1=ADD
     )
-    rms = work.tile([P, 2, HEADS], F32)
+    rms = work.tile([P, HEADS], F32, name="rms%d" % s)
     nc.scalar.activation(out=rms[:], in_=mean_eps[:], func=SQRT)
-    k_part = products(1, 0)
-    rrms = work.tile([P, 2, HEADS], F32)
+    rrms = work.tile([P, HEADS], F32, name="rrms%d" % s)
     nc.vector.reciprocal(out=rrms[:], in_=rms[:])
-    normalise(0, q_rows)
-    k_rows = mix(1, k_part, products(1, 1))
-    normalise(1, k_rows)
-    return q_rows, k_rows
+    nc.vector.tensor_tensor(
+        out=rows, in0=rows, in1=rrms[:].unsqueeze(2).to_broadcast([P, HEADS, FEATURES]), op=MULT
+    )
+    return rows
 
 
 def features_to_partitions(nc, work, psum, ident, rows, s):
@@ -321,9 +309,17 @@ def tile_selfattention_pa_k_kernel(
         bias_planes, bias_v, tables = spread_constants(nc, keep, psum, row, pe_sb)
 
         acc_qk = open_banks(psum, QK_COLS)
-        for g in range(GROUPS):
+        for g in range(GROUPS - SPLIT_GROUPS):
             multiply_group(nc, w_qk_pool, acc_qk, qkv_w_words, w_planes, x_codes, x_planes, 0, g)
-        q_rows, k_rows = norm_and_rotate(nc, work, acc_qk, bias_planes, tables)
+        rows = []
+        for s in range(2):
+            acc = acc_qk[s * BANKS_PER_STREAM : (s + 1) * BANKS_PER_STREAM]
+            for g in range(GROUPS - SPLIT_GROUPS, GROUPS):
+                multiply_group(
+                    nc, w_qk_pool, acc, qkv_w_words, w_planes, x_codes, x_planes, s * STREAM_COLS, g
+                )
+            rows.append(norm_and_rotate(nc, work, acc, bias_planes, tables, s))
+        q_rows, k_rows = rows
 
         acc_v = open_banks(psum_v, STREAM_COLS)
         for g in range(GROUPS - SPLIT_GROUPS):

from contextlib import ExitStack

import concourse.mybir as mybir
from concourse.masks import make_identity

BF16 = mybir.dt.bfloat16
F32 = mybir.dt.float32
I32 = mybir.dt.int32
U32 = mybir.dt.uint32
U8 = mybir.dt.uint8
FP8X4 = mybir.dt.float8_e4m3fn_x4
ADD = mybir.AluOpType.add
MULT = mybir.AluOpType.mult
SQUARE = mybir.ActivationFunctionType.Square
SQRT = mybir.ActivationFunctionType.Sqrt

P = 128
BATCHES = 2
POSITIONS = 64
HEADS = 16
FEATURES = 64
PAIRS = FEATURES // 2
EPS = 1e-6

PACK = 4
K_GROUP = P * PACK
K_ALL = 8192
GROUPS = K_ALL // K_GROUP
WORDS_PER_GROUP = K_GROUP // 2

STREAM_COLS = HEADS * FEATURES
QK_COLS = 2 * STREAM_COLS
N_ALL = 3 * STREAM_COLS
BANK = 512
BANKS_PER_STREAM = STREAM_COLS // BANK
HEADS_PER_BANK = BANK // FEATURES
PSUM_BANKS = 8

X_CHUNKS = 4
CHUNK_GROUPS = GROUPS // X_CHUNKS
CHUNK_K = K_ALL // X_CHUNKS
X_LOADS = 2
X_LOAD_K = K_ALL // X_LOADS

RUN = 8
Q_TURN_1, Q_TURN_2, K_TURN_1, K_TURN_2 = 2, 8, 7, 9
SPLIT_GROUPS = 4

PLANES_PER_TILE = 4
QK_BUFS = 8
V_BUFS = 12

ROW_COLS = N_ALL + BANK

FLOPS = 2 * P * K_ALL * N_ALL


def load_small_inputs(nc, keep, pe, qkv_b, q_scale, k_scale):
    row = keep.tile([P, ROW_COLS], BF16)
    nc.vector.memset(row[:].bitcast(I32), 0)
    nc.scalar.dma_start(out=row[0:1, 0:N_ALL], in_=qkv_b.rearrange("(o n) -> o n", o=1))
    nc.scalar.dma_start(out=row[0:1, N_ALL : N_ALL + FEATURES], in_=q_scale.rearrange("(o n) -> o n", o=1))
    nc.scalar.dma_start(
        out=row[0:1, N_ALL + FEATURES : N_ALL + 2 * FEATURES], in_=k_scale.rearrange("(o n) -> o n", o=1)
    )
    pe_sb = keep.tile([P, PAIRS * 4], BF16)
    for b in range(BATCHES):
        nc.scalar.dma_start(
            out=pe_sb[b:P:BATCHES, :],
            in_=pe.rearrange("a b l i r c -> (a b l) (i r c)"),
        )
    return row, pe_sb


def load_x(nc, x_pool, x):
    x_chunks = []
    for c in range(X_LOADS):
        x_half = x_pool.tile([P, X_LOAD_K], BF16)
        for b in range(BATCHES):
            nc.sync.dma_start(out=x_half[b:P:BATCHES, :], in_=x[b, :, c * X_LOAD_K : (c + 1) * X_LOAD_K])
        for i in range(X_LOAD_K // CHUNK_K):
            x_chunks.append(x_half[:, i * CHUNK_K : (i + 1) * CHUNK_K])
    return x_chunks


def load_w_scales(nc, w_planes, qkv_w_scales):
    for j in range(GROUPS // PLANES_PER_TILE):
        for quadrant in range(4):
            nc.gpsimd.dma_start(
                out=w_planes[32 * quadrant : 32 * quadrant + 16, j, :].bitcast(F32),
                in_=qkv_w_scales[
                    PLANES_PER_TILE * j : PLANES_PER_TILE * (j + 1), 4 * quadrant : 4 * quadrant + 4, :
                ].bitcast(F32),
            )


def quantise_x(nc, keep, grouped_pool, psum, ident, x_chunks):
    x_codes = keep.tile([P, GROUPS, P], U32, align_bytes=64)
    x_planes = keep.tile([P, GROUPS, P], U8, align_bytes=64)
    for c in range(X_CHUNKS):
        x_words = x_chunks[c].bitcast(F32)
        grouped = grouped_pool.tile([P, CHUNK_GROUPS, P, PACK], BF16, align_bytes=64)
        grouped_words = grouped[:].bitcast(F32)
        for half in range(2):
            turned = psum.tile([P, 2, 2, P], F32, tag="bank")
            for gl in range(2):
                first = WORDS_PER_GROUP * (2 * half + gl)
                for u in range(2):
                    nc.tensor.transpose(
                        turned[:, gl, u, :], x_words[:, first + u : first + WORDS_PER_GROUP : 2], ident[:]
                    )
            side_by_side = turned[:].rearrange("p g u m -> p g m u")
            if half == 0:
                nc.vector.tensor_copy(out=grouped_words[:, 0:2, :, :], in_=side_by_side)
            else:
                nc.scalar.copy(out=grouped_words[:, 2:4, :, :], in_=side_by_side)
        groups = slice(c * CHUNK_GROUPS, (c + 1) * CHUNK_GROUPS)
        nc.vector.quantize_mx(
            out=x_codes[:, groups, :].rearrange("p g m -> p (g m)").bitcast(FP8X4),
            scales=x_planes[:, groups, :].rearrange("p g m -> p (g m)"),
            in_=grouped[:].rearrange("p g m t -> p (g m t)"),
        )
    return x_codes, x_planes


def spread_constants(nc, keep, psum, row, pe_sb):
    ones = keep.tile([P, P], BF16)
    nc.vector.memset(ones[:], 1.0)
    bias_planes = keep.tile([P, 2, 2, HEADS, PAIRS], F32)
    bias_v = keep.tile([P, STREAM_COLS], F32)
    tables = keep.tile([P, 2, 2, 2, PAIRS], F32)
    for t in range(ROW_COLS // BANK):
        spread = psum.tile([P, BANK], F32, tag="bank")
        nc.tensor.matmul(out=spread[:], lhsT=ones[:], rhs=row[:, t * BANK : (t + 1) * BANK], start=True, stop=True)
        stream = t // BANKS_PER_STREAM
        j = t % BANKS_PER_STREAM
        if stream < 2:
            nc.scalar.copy(
                out=bias_planes[:, stream, :, j * HEADS_PER_BANK : (j + 1) * HEADS_PER_BANK, :],
                in_=spread[:].rearrange("p (h i e) -> p e h i", i=PAIRS, e=2),
            )
        elif stream == 2:
            nc.scalar.copy(out=bias_v[:, j * BANK : (j + 1) * BANK], in_=spread[:])
        else:
            for s in range(2):
                gain = spread[:, s * FEATURES : (s + 1) * FEATURES].rearrange("p (i c) -> p c i", c=2)
                nc.vector.tensor_tensor(
                    out=tables[:, s],
                    in0=pe_sb[:].rearrange("p (i r c) -> p c r i", r=2, c=2),
                    in1=gain.unsqueeze(2).to_broadcast([P, 2, 2, PAIRS]),
                    op=MULT,
                )
    return bias_planes, bias_v, tables


def open_banks(pool, n_cols):
    acc = []
    for j in range(n_cols // BANK):
        bank = pool.tile([P, BANK], F32, tag="bank")
        acc.append(bank)
    return acc


def multiply_group(nc, w_pool, acc, qkv_w_words, w_planes, x_codes, x_planes, first_col, g):
    n_cols = len(acc) * BANK
    w_words = w_pool.tile([P, n_cols], U32, align_bytes=64)
    nc.sync.dma_start(
        out=w_words[:].bitcast(I32),
        in_=qkv_w_words[g]
        .rearrange("p n t -> p (n t)")[:, PACK * first_col : PACK * (first_col + n_cols)]
        .bitcast(I32),
    )
    plane_start = 4 * (g % PLANES_PER_TILE)
    for j in range(n_cols // BANK):
        nc.tensor.matmul_mx(
            out=acc[j][:],
            lhsT=x_codes[:, g, :].bitcast(FP8X4),
            lhsT_scale=x_planes[:, g, :],
            rhs=w_words[:, j * BANK : (j + 1) * BANK].bitcast(FP8X4),
            rhs_scale=w_planes[
                plane_start:P, g // PLANES_PER_TILE, first_col + j * BANK : first_col + (j + 1) * BANK
            ],
            start=(g == 0),
            stop=(g == GROUPS - 1),
        )


def store_heads(nc, out_dram, heads, rows):
    for b in range(BATCHES):
        nc.sync.dma_start(
            out=out_dram[b, heads].rearrange("h l d -> l h d"),
            in_=rows[b:P:BATCHES],
        )


def norm_and_rotate(nc, work, acc, bias_planes, tables, s):
    planes_shape = [P, 2, HEADS, PAIRS]
    biased = work.tile(planes_shape, F32, name="biased%d" % s)
    for j in range(BANKS_PER_STREAM):
        heads = slice(j * HEADS_PER_BANK, (j + 1) * HEADS_PER_BANK)
        nc.vector.tensor_tensor(
            out=biased[:].rearrange("p e (c a) i -> p e c a i", a=2)[:, :, :, j, :],
            in0=acc[j][:].rearrange("p (h i e) -> p e h i", i=PAIRS, e=2),
            in1=bias_planes[:, s, :, heads, :],
            op=ADD,
        )

    sums = work.tile([P, HEADS], F32, name="sums%d" % s)
    squares = work.tile(planes_shape, F32)
    for h in range(HEADS):
        nc.scalar.activation(
            out=squares[:, :, h, :], in_=biased[:, :, h, :], func=SQUARE, accum_out=sums[:, h : h + 1]
        )

    from_plane = []
    for c in range(2):
        part = work.tile(planes_shape, F32, name="from_plane%d" % c)
        nc.vector.tensor_tensor(
            out=part[:],
            in0=biased[:, c].unsqueeze(1).to_broadcast(planes_shape),
            in1=tables[:, s, c].unsqueeze(2).to_broadcast(planes_shape),
            op=MULT,
        )
        from_plane.append(part)
    mixed = work.tile([P, HEADS, PAIRS, 2], F32, name="rotated%d" % s)
    nc.vector.tensor_tensor(
        out=mixed[:],
        in0=from_plane[0][:].rearrange("p r h i -> p h i r"),
        in1=from_plane[1][:].rearrange("p r h i -> p h i r"),
        op=ADD,
    )
    rows = mixed[:].rearrange("p h i r -> p h (i r)")

    mean_eps = work.tile([P, HEADS], F32, name="mean_eps%d" % s)
    nc.vector.tensor_scalar(
        out=mean_eps[:], in0=sums[:], scalar1=1.0 / FEATURES, scalar2=EPS, op0=MULT, op1=ADD
    )
    rms = work.tile([P, HEADS], F32, name="rms%d" % s)
    nc.scalar.activation(out=rms[:], in_=mean_eps[:], func=SQRT)
    rrms = work.tile([P, HEADS], F32, name="rrms%d" % s)
    nc.vector.reciprocal(out=rrms[:], in_=rms[:])
    nc.vector.tensor_tensor(
        out=rows, in0=rows, in1=rrms[:].unsqueeze(2).to_broadcast([P, HEADS, FEATURES]), op=MULT
    )
    return rows


def features_to_partitions(nc, work, psum, ident, rows, s):
    flat = rows.rearrange("p h d -> p (h d)")
    columns = work.tile([P, RUN, P], F32, name="columns%d" % s)
    for half in range(2):
        bank = psum.tile([P, 4, P], F32, tag="bank")
        for i in range(4):
            c = 4 * half + i
            nc.tensor.transpose(bank[:, i, :], flat[:, c * P : (c + 1) * P], ident[:])
        nc.scalar.copy(
            out=columns[:, :, half * 64 : (half + 1) * 64].rearrange("p t (q b) -> p t q b", b=BATCHES),
            in_=bank[:].rearrange("p c (m t b) -> p t (c m) b", t=RUN, b=BATCHES),
        )
    return columns


def positions_to_partitions(nc, work, psum, ident, columns, s):
    runs = work.tile([P, 2, RUN, FEATURES], F32, name="runs%d" % s)
    for half in range(2):
        bank = psum.tile([P, 4, P], F32, tag="bank")
        for i in range(4):
            nc.tensor.transpose(bank[:, i, :], columns[:, 4 * half + i, :], ident[:])
        nc.scalar.copy(
            out=runs[:, :, 4 * half : 4 * half + 4, :], in_=bank[:].rearrange("p t (a d) -> p a t d", a=2)
        )
    return runs


def store_runs(nc, out_dram, runs):
    for b in range(BATCHES):
        nc.sync.dma_start(
            out=out_dram[b].rearrange("(a c) (m t) d -> (c m) a (t d)", a=2, t=RUN),
            in_=runs[b:P:BATCHES].rearrange("p a t d -> p a (t d)"),
        )


def tile_selfattention_pa_k_kernel(
    tc, x, pe, qkv_w_words, qkv_w_scales, qkv_b, q_scale, k_scale, out_0, out_1, out_2
):
    nc = tc.nc
    with ExitStack() as ctx:
        ctx.enter_context(tc.manual_schedule())
        keep = ctx.enter_context(tc.tile_pool(name="keep", bufs=1))
        x_pool = ctx.enter_context(tc.tile_pool(name="x_pool", bufs=X_LOADS))
        grouped_pool = ctx.enter_context(tc.tile_pool(name="grouped_pool", bufs=2))
        w_qk_pool = ctx.enter_context(tc.tile_pool(name="w_qk_pool", bufs=QK_BUFS))
        w_v_pool = ctx.enter_context(tc.tile_pool(name="w_v_pool", bufs=V_BUFS))
        work = ctx.enter_context(tc.tile_pool(name="work", bufs=1))
        psum = ctx.enter_context(tc.psum_pool(name="psum", bufs=PSUM_BANKS - BANKS_PER_STREAM))
        psum_v = ctx.enter_context(tc.psum_pool(name="psum_v", bufs=BANKS_PER_STREAM))

        ident = keep.tile([P, P], F32)
        make_identity(nc, ident[:])
        w_planes = keep.tile([P, GROUPS // PLANES_PER_TILE, N_ALL], U8, align_bytes=64)
        nc.vector.memset(w_planes[:, 0, :].bitcast(I32), 0)
        x_chunks = load_x(nc, x_pool, x)
        row, pe_sb = load_small_inputs(nc, keep, pe, qkv_b, q_scale, k_scale)
        for j in range(1, GROUPS // PLANES_PER_TILE):
            nc.vector.memset(w_planes[:, j, :].bitcast(I32), 0)

        load_w_scales(nc, w_planes, qkv_w_scales)
        x_codes, x_planes = quantise_x(nc, keep, grouped_pool, psum, ident, x_chunks)
        bias_planes, bias_v, tables = spread_constants(nc, keep, psum, row, pe_sb)

        acc_qk = open_banks(psum, QK_COLS)
        for g in range(GROUPS - SPLIT_GROUPS):
            multiply_group(nc, w_qk_pool, acc_qk, qkv_w_words, w_planes, x_codes, x_planes, 0, g)
        rows = []
        for s in range(2):
            acc = acc_qk[s * BANKS_PER_STREAM : (s + 1) * BANKS_PER_STREAM]
            for g in range(GROUPS - SPLIT_GROUPS, GROUPS):
                multiply_group(
                    nc, w_qk_pool, acc, qkv_w_words, w_planes, x_codes, x_planes, s * STREAM_COLS, g
                )
            rows.append(norm_and_rotate(nc, work, acc, bias_planes, tables, s))
        q_rows, k_rows = rows

        acc_v = open_banks(psum_v, STREAM_COLS)
        for g in range(GROUPS - SPLIT_GROUPS):
            multiply_group(nc, w_v_pool, acc_v, qkv_w_words, w_planes, x_codes, x_planes, QK_COLS, g)
            if g == Q_TURN_1:
                q_columns = features_to_partitions(nc, work, psum, ident, q_rows, 0)
            elif g == Q_TURN_2:
                q_runs = positions_to_partitions(nc, work, psum, ident, q_columns, 0)
            elif g == K_TURN_1:
                k_columns = features_to_partitions(nc, work, psum, ident, k_rows, 1)
            elif g == K_TURN_2:
                k_runs = positions_to_partitions(nc, work, psum, ident, k_columns, 1)
        for j in range(BANKS_PER_STREAM):
            for g in range(GROUPS - SPLIT_GROUPS, GROUPS):
                first_col = QK_COLS + j * BANK
                multiply_group(
                    nc, w_v_pool, acc_v[j : j + 1], qkv_w_words, w_planes, x_codes, x_planes, first_col, g
                )
        store_runs(nc, out_0, q_runs)
        store_runs(nc, out_1, k_runs)

        for j in range(BANKS_PER_STREAM):
            v_rows = work.tile([P, BANK], F32, name="v_rows%d" % j)
            nc.vector.tensor_tensor(out=v_rows[:], in0=acc_v[j][:], in1=bias_v[:, j * BANK : (j + 1) * BANK], op=ADD)
            store_heads(
                nc,
                out_2,
                slice(j * HEADS_PER_BANK, (j + 1) * HEADS_PER_BANK),
                v_rows[:].rearrange("p (h d) -> p h d", d=FEATURES),
            )
